import numpy as np
import ml_dtypes


def mxq(x, axis, fmt="e4m3"):
    dtype, down = {"e4m3": (ml_dtypes.float8_e4m3fn, 7), "e5m2": (ml_dtypes.float8_e5m2, 14)}[fmt]
    v = np.moveaxis(np.asarray(x, np.float32).astype(ml_dtypes.bfloat16).astype(np.float64), axis, -1)
    blocks = v.reshape(v.shape[:-1] + (-1, 32))
    amax = np.abs(blocks).max(-1, keepdims=True)
    byte = np.maximum(np.where(amax > 0, np.frexp(amax)[1] - 1 + 127, 0) - down, 1)
    scale = np.exp2(byte - 127.0)
    codes = (blocks / scale).astype(np.float32).astype(dtype).astype(np.float64)
    return np.moveaxis((codes * scale).reshape(v.shape), -1, axis)


WIDE = False


def mx_kscale(k):
    if not WIDE:
        return np.ones(k)
    levels = np.array([20, -20, 10, -10, 0])
    a = np.random.permutation(np.resize(levels, k // 512 * 4)).reshape(k // 512, 4)
    idx = np.arange(k)
    return np.exp2(a[idx // 512, idx % 128 // 32])


BF16 = ml_dtypes.bfloat16


def bf(x):
    return np.asarray(x, np.float32).astype(BF16)


def f64(x):
    return np.asarray(x).astype(np.float64)


B, C_IN, C_OUT, K, H, W = 2, 1024, 512, 3, 32, 32


def _shift2d(x, dh, dw):
    hh, ww = x.shape[2], x.shape[3]
    ph, pw = abs(dh), abs(dw)
    xp = np.pad(x, ((0, 0), (0, 0), (ph, ph), (pw, pw)))
    return xp[:, :, ph + dh: ph + dh + hh, pw + dw: pw + dw + ww]


def setup_inputs():
    u = mx_kscale(C_OUT)
    bound = np.sqrt(2.0) * np.sqrt(3.0 / (C_IN * K))
    x = np.random.standard_normal((B, C_IN, H, W))
    weight = np.random.uniform(-bound, bound, (C_OUT, C_IN, K)) / u[:, None, None]
    g = (np.random.standard_normal((B, C_OUT, H, W))
         * np.exp2(np.random.randint(-12, 1, (B, 1, H, W))) * 4.0 * u[None, :, None, None])
    return {"x": bf(x), "weight": bf(weight), "dilation": 1, "step": 1, "grad_out": bf(g)}


def reference(x, weight, dilation, step, grad_out):
    nb, no, nh, nw = grad_out.shape
    nc_in, nk = weight.shape[1], weight.shape[2]
    c0 = nk // 2
    gq = mxq(f64(grad_out).reshape(nb, no, nh * nw), 1, "e5m2")
    out = np.zeros((nb, nc_in, nh, nw))
    for k in range(nk):
        off = k - c0
        y = mxq(f64(weight)[:, :, k], 0, "e4m3").T @ gq
        out = out + _shift2d(y.reshape(nb, nc_in, nh, nw), -off * step, -off * dilation)
    return out

@@ -1,0 +1,181 @@
+from contextlib import ExitStack
+
+import concourse.mybir as mybir
+
+BF16 = mybir.dt.bfloat16
+F32 = mybir.dt.float32
+U32 = mybir.dt.uint32
+U8 = mybir.dt.uint8
+E4M3_X4 = mybir.dt.float8_e4m3fn_x4
+E5M2_X4 = mybir.dt.float8_e5m2_x4
+
+P = 128
+PACK = 4
+BATCHES, C_IN, C_OUT, TAPS, HEIGHT, WIDTH = 2, 1024, 512, 3, 32, 32
+CENTRE = TAPS // 2
+POSITIONS = HEIGHT * WIDTH
+N_TILE = 512
+ROWS_TILE = N_TILE // WIDTH
+HALVES = POSITIONS // N_TILE
+C_TILE = P
+C_TILES = C_IN // C_TILE
+C_CHUNK = 2 * C_TILE
+C_CHUNKS = C_IN // C_CHUNK
+C_CHUNK_SCALAR = 3 * C_CHUNK // 4
+PSUM_BANKS = 8
+VECTOR_EMPTIES_EVERY = 4
+STAGING_BUFS = 6
+
+FLOPS = 2 * BATCHES * C_IN * POSITIONS * C_OUT * TAPS
+BYTES = 2 * C_OUT * C_IN * TAPS + 2 * BATCHES * C_OUT * POSITIONS + 4 * BATCHES * C_IN * POSITIONS
+
+
+def inside(first, count, shift, size):
+    return max(first, shift), min(first + count, size + shift)
+
+
+def tile_skeletonconv_t_kernel(tc, x, weight, dilation, step, grad_out, out):
+    nc = tc.nc
+    assert tuple(grad_out.shape) == (BATCHES, C_OUT, HEIGHT, WIDTH)
+    assert tuple(weight.shape) == (C_OUT, C_IN, TAPS)
+    assert C_OUT == P * PACK
+
+    grad_rows = grad_out.rearrange("b (p j) h w -> b p j (h w)", j=PACK)
+    weight_rows = weight.rearrange("(p j) c k -> p j (c k)", j=PACK)
+    out_rows = out.rearrange("b c h w -> b c (h w)")
+
+    with ExitStack() as ctx:
+        keep = ctx.enter_context(tc.tile_pool(name="keep", bufs=1))
+        staging = ctx.enter_context(tc.tile_pool(name="staging", bufs=STAGING_BUFS))
+        psum = ctx.enter_context(tc.psum_pool(name="psum", bufs=PSUM_BANKS))
+
+        g_raw = [keep.tile([P, PACK, POSITIONS], BF16, name="g_raw%d" % b) for b in range(BATCHES)]
+        w_raw = [
+            keep.tile([P, PACK, C_CHUNK * TAPS], BF16, name="w_raw%d" % cc) for cc in range(C_CHUNKS)
+        ]
+        g_tap = [
+            keep.tile([P, BATCHES, HEIGHT, WIDTH, PACK], BF16, name="g_tap%d" % k, align_bytes=64)
+            for k in range(TAPS)
+        ]
+        g_codes = [
+            keep.tile([P, BATCHES * POSITIONS], U32, name="g_codes%d" % k, align_bytes=64)
+            for k in range(TAPS)
+        ]
+        g_scales = [
+            keep.tile([P, BATCHES * POSITIONS], U8, name="g_scales%d" % k, align_bytes=64)
+            for k in range(TAPS)
+        ]
+        w_grouped = [
+            keep.tile([P, TAPS, C_CHUNK, PACK], BF16, name="w_grouped%d" % cc, align_bytes=64)
+            for cc in range(C_CHUNKS)
+        ]
+        w_codes = keep.tile([P, TAPS, C_IN], U32, align_bytes=64)
+        w_scales = keep.tile([P, TAPS, C_IN], U8, align_bytes=64)
+
+        def load_inputs():
+            nc.sync.dma_start(out=g_raw[0][:], in_=grad_rows[0])
+            for cc in range(C_CHUNKS):
+                columns = slice(cc * C_CHUNK * TAPS, (cc + 1) * C_CHUNK * TAPS)
+                nc.sync.dma_start(out=w_raw[cc][:], in_=weight_rows[:, :, columns])
+            for b in range(1, BATCHES):
+                nc.sync.dma_start(out=g_raw[b][:], in_=grad_rows[b])
+
+        def zero_outside_the_map():
+            for k in range(TAPS):
+                row_lo, row_hi = inside(0, HEIGHT, (k - CENTRE) * step, HEIGHT)
+                col_lo, col_hi = inside(0, WIDTH, (k - CENTRE) * dilation, WIDTH)
+                for lo, hi in ((0, row_lo), (row_hi, HEIGHT)):
+                    if lo < hi:
+                        nc.vector.memset(g_tap[k][:, :, lo:hi, :, :], 0.0)
+                for lo, hi in ((0, col_lo), (col_hi, WIDTH)):
+                    if lo < hi:
+                        nc.vector.memset(g_tap[k][:, :, :, lo:hi, :], 0.0)
+
+        def regroup_grad(b):
+            for half in range(HALVES):
+                engine_copy = nc.vector.tensor_copy if half == 0 else nc.scalar.copy
+                rows = slice(half * ROWS_TILE, (half + 1) * ROWS_TILE)
+                positions = slice(half * N_TILE, (half + 1) * N_TILE)
+                engine_copy(
+                    out=g_tap[CENTRE][:, b, rows, :, :].rearrange("p h (q i) j -> p (h q) j i", i=4),
+                    in_=g_raw[b][:, :, positions].rearrange("p j (q i) -> p q j i", i=4),
+                )
+
+        def quantise_grad(k, b, half):
+            rows = slice(half * ROWS_TILE, (half + 1) * ROWS_TILE)
+            columns = slice(b * POSITIONS + half * N_TILE, b * POSITIONS + (half + 1) * N_TILE)
+            nc.vector.quantize_mx(
+                out=g_codes[k][:, columns].bitcast(E5M2_X4),
+                scales=g_scales[k][:, columns],
+                in_=g_tap[k][:, b, rows, :, :].rearrange("p h w j -> p (h w j)"),
+            )
+
+        def shift_grad(k, b, half):
+            down, right = (k - CENTRE) * step, (k - CENTRE) * dilation
+            row_lo, row_hi = inside(half * ROWS_TILE, ROWS_TILE, down, HEIGHT)
+            col_lo, col_hi = inside(0, WIDTH, right, WIDTH)
+            nc.vector.tensor_copy(
+                out=g_tap[k][:, b, row_lo:row_hi, col_lo:col_hi, :],
+                in_=g_tap[CENTRE][:, b, row_lo - down : row_hi - down, col_lo - right : col_hi - right, :],
+            )
+
+        def prepare_grad(b, half):
+            if half == 0:
+                regroup_grad(b)
+            for k in range(TAPS):
+                if k != CENTRE:
+                    shift_grad(k, b, half)
+            for k in range(TAPS):
+                quantise_grad(k, b, half)
+
+        def prepare_weight(cc):
+            for engine_copy, cols in (
+                (nc.scalar.copy, slice(0, C_CHUNK_SCALAR)),
+                (nc.vector.tensor_copy, slice(C_CHUNK_SCALAR, C_CHUNK)),
+            ):
+                engine_copy(
+                    out=w_grouped[cc][:, :, cols, :],
+                    in_=w_raw[cc][:].rearrange("p j (c k) -> p k c j", k=TAPS)[:, :, cols, :],
+                )
+            columns = slice(cc * C_CHUNK, (cc + 1) * C_CHUNK)
+            for k in range(TAPS):
+                nc.vector.quantize_mx(
+                    out=w_codes[:, k, columns].bitcast(E4M3_X4),
+                    scales=w_scales[:, k, columns],
+                    in_=w_grouped[cc][:, k, :, :].rearrange("p c j -> p (c j)"),
+                )
+
+        def multiply(b, half):
+            columns = slice(b * POSITIONS + half * N_TILE, b * POSITIONS + (half + 1) * N_TILE)
+            for ct in range(C_TILES):
+                channels = slice(ct * C_TILE, (ct + 1) * C_TILE)
+                acc = psum.tile([C_TILE, N_TILE], F32)
+                for k in range(TAPS):
+                    nc.tensor.matmul_mx(
+                        out=acc[:],
+                        lhsT=w_codes[:, k, channels].bitcast(E4M3_X4),
+                        lhsT_scale=w_scales[:, k, channels],
+                        rhs=g_codes[k][:, columns].bitcast(E5M2_X4),
+                        rhs_scale=g_scales[k][:, columns],
+                        start=(k == 0),
+                        stop=(k == TAPS - 1),
+                    )
+                result = staging.tile([C_TILE, N_TILE], F32)
+                if ct % VECTOR_EMPTIES_EVERY == VECTOR_EMPTIES_EVERY - 1:
+                    nc.vector.tensor_copy(out=result[:], in_=acc[:])
+                else:
+                    nc.scalar.copy(out=result[:], in_=acc[:])
+                nc.sync.dma_start(
+                    out=out_rows[b, channels, half * N_TILE : (half + 1) * N_TILE], in_=result[:]
+                )
+
+        half_maps = [(b, half) for b in range(BATCHES) for half in range(HALVES)]
+        load_inputs()
+        zero_outside_the_map()
+        prepare_grad(*half_maps[0])
+        for cc in range(C_CHUNKS):
+            prepare_weight(cc)
+        for i in range(len(half_maps)):
+            if i + 1 < len(half_maps):
+                prepare_grad(*half_maps[i + 1])
+            multiply(*half_maps[i])

@@ -134,8 +134,8 @@ def tile_skeletonconv_t_kernel(tc, x, weight, dilation, step, grad_out, out):
                 (nc.vector.tensor_copy, slice(C_CHUNK_SCALAR, C_CHUNK)),
             ):
                 engine_copy(
-                    out=w_grouped[cc][:, :, cols, :],
-                    in_=w_raw[cc][:].rearrange("p j (c k) -> p k c j", k=TAPS)[:, :, cols, :],
+                    out=w_grouped[cc][:, :, cols, :].rearrange("p k c j -> p c j k"),
+                    in_=w_raw[cc][:].rearrange("p j (c k) -> p c j k", k=TAPS)[:, cols, :, :],
                 )
             columns = slice(cc * C_CHUNK, (cc + 1) * C_CHUNK)
             for k in range(TAPS):

@@ -21,7 +21,7 @@ C_TILE = P
 C_TILES = C_IN // C_TILE
 C_CHUNK = 2 * C_TILE
 C_CHUNKS = C_IN // C_CHUNK
-C_CHUNK_SCALAR = 3 * C_CHUNK // 4
+C_CHUNK_SCALAR = 5 * C_CHUNK // 8
 PSUM_BANKS = 8
 VECTOR_EMPTIES_EVERY = 4
 STAGING_BUFS = 6
@@ -39,6 +39,9 @@ def tile_skeletonconv_t_kernel(tc, x, weight, dilation, step, grad_out, out):
     assert tuple(grad_out.shape) == (BATCHES, C_OUT, HEIGHT, WIDTH)
     assert tuple(weight.shape) == (C_OUT, C_IN, TAPS)
     assert C_OUT == P * PACK
+
+    upper_rows = ROWS_TILE + CENTRE * step
+    row_parts = ((0, upper_rows), (upper_rows, HEIGHT))
 
     grad_rows = grad_out.rearrange("b (p j) h w -> b p j (h w)", j=PACK)
     weight_rows = weight.rearrange("(p j) c k -> p j (c k)", j=PACK)
@@ -72,13 +75,18 @@ def tile_skeletonconv_t_kernel(tc, x, weight, dilation, step, grad_out, out):
         w_codes = keep.tile([P, TAPS, C_IN], U32, align_bytes=64)
         w_scales = keep.tile([P, TAPS, C_IN], U8, align_bytes=64)
 
+        def load_grad(b):
+            for first, end in row_parts:
+                positions = slice(first * WIDTH, end * WIDTH)
+                nc.sync.dma_start(out=g_raw[b][:, :, positions], in_=grad_rows[b][:, :, positions])
+
         def load_inputs():
-            nc.sync.dma_start(out=g_raw[0][:], in_=grad_rows[0])
+            load_grad(0)
             for cc in range(C_CHUNKS):
                 columns = slice(cc * C_CHUNK * TAPS, (cc + 1) * C_CHUNK * TAPS)
                 nc.sync.dma_start(out=w_raw[cc][:], in_=weight_rows[:, :, columns])
             for b in range(1, BATCHES):
-                nc.sync.dma_start(out=g_raw[b][:], in_=grad_rows[b])
+                load_grad(b)
 
         def zero_outside_the_map():
             for k in range(TAPS):
@@ -92,13 +100,14 @@ def tile_skeletonconv_t_kernel(tc, x, weight, dilation, step, grad_out, out):
                         nc.vector.memset(g_tap[k][:, :, :, lo:hi, :], 0.0)
 
         def regroup_grad(b):
-            for half in range(HALVES):
-                engine_copy = nc.vector.tensor_copy if half == 0 else nc.scalar.copy
-                rows = slice(half * ROWS_TILE, (half + 1) * ROWS_TILE)
-                positions = slice(half * N_TILE, (half + 1) * N_TILE)
+            for engine_copy, (first, end) in zip((nc.vector.tensor_copy, nc.scalar.copy), row_parts):
                 engine_copy(
-                    out=g_tap[CENTRE][:, b, rows, :, :].rearrange("p h (q i) j -> p (h q) j i", i=4),
-                    in_=g_raw[b][:, :, positions].rearrange("p j (q i) -> p q j i", i=4),
+                    out=g_tap[CENTRE][:, b, first:end, :, :].rearrange(
+                        "p h (q i) j -> p (h q) j i", i=4
+                    ),
+                    in_=g_raw[b][:, :, first * WIDTH : end * WIDTH].rearrange(
+                        "p j (q i) -> p q j i", i=4
+                    ),
                 )
 
         def quantise_grad(k, b, half):

@@ -23,7 +23,6 @@ C_CHUNK = 2 * C_TILE
 C_CHUNKS = C_IN // C_CHUNK
 C_CHUNK_SCALAR = 5 * C_CHUNK // 8
 PSUM_BANKS = 8
-VECTOR_EMPTIES_EVERY = 4
 STAGING_BUFS = 6
 
 FLOPS = 2 * BATCHES * C_IN * POSITIONS * C_OUT * TAPS
@@ -51,8 +50,15 @@ def tile_skeletonconv_t_kernel(tc, x, weight, dilation, step, grad_out, out):
         keep = ctx.enter_context(tc.tile_pool(name="keep", bufs=1))
         staging = ctx.enter_context(tc.tile_pool(name="staging", bufs=STAGING_BUFS))
         psum = ctx.enter_context(tc.psum_pool(name="psum", bufs=PSUM_BANKS))
+        ctx.enter_context(tc.manual_schedule())
 
-        g_raw = [keep.tile([P, PACK, POSITIONS], BF16, name="g_raw%d" % b) for b in range(BATCHES)]
+        g_raw = [
+            [
+                keep.tile([P, PACK, (end - first) * WIDTH], BF16, name="g_raw%d_%d" % (b, first))
+                for first, end in row_parts
+            ]
+            for b in range(BATCHES)
+        ]
         w_raw = [
             keep.tile([P, PACK, C_CHUNK * TAPS], BF16, name="w_raw%d" % cc) for cc in range(C_CHUNKS)
         ]
@@ -75,10 +81,17 @@ def tile_skeletonconv_t_kernel(tc, x, weight, dilation, step, grad_out, out):
         w_codes = keep.tile([P, TAPS, C_IN], U32, align_bytes=64)
         w_scales = keep.tile([P, TAPS, C_IN], U8, align_bytes=64)
 
+        def wake_scalar():
+            column = keep.tile([P, 1], F32)
+            column_copy = keep.tile([P, 1], F32)
+            nc.vector.memset(column[:], 0.0)
+            nc.scalar.copy(out=column_copy[:], in_=column[:])
+
         def load_grad(b):
-            for first, end in row_parts:
-                positions = slice(first * WIDTH, end * WIDTH)
-                nc.sync.dma_start(out=g_raw[b][:, :, positions], in_=grad_rows[b][:, :, positions])
+            for part, (first, end) in enumerate(row_parts):
+                nc.sync.dma_start(
+                    out=g_raw[b][part][:], in_=grad_rows[b][:, :, first * WIDTH : end * WIDTH]
+                )
 
         def load_inputs():
             load_grad(0)
@@ -100,14 +113,13 @@ def tile_skeletonconv_t_kernel(tc, x, weight, dilation, step, grad_out, out):
                         nc.vector.memset(g_tap[k][:, :, :, lo:hi, :], 0.0)
 
         def regroup_grad(b):
-            for engine_copy, (first, end) in zip((nc.vector.tensor_copy, nc.scalar.copy), row_parts):
+            for part, (first, end) in enumerate(row_parts):
+                engine_copy = nc.vector.tensor_copy if part == 0 else nc.scalar.copy
                 engine_copy(
                     out=g_tap[CENTRE][:, b, first:end, :, :].rearrange(
                         "p h (q i) j -> p (h q) j i", i=4
                     ),
-                    in_=g_raw[b][:, :, first * WIDTH : end * WIDTH].rearrange(
-                        "p j (q i) -> p q j i", i=4
-                    ),
+                    in_=g_raw[b][part][:].rearrange("p j (q i) -> p q j i", i=4),
                 )
 
         def quantise_grad(k, b, half):
@@ -154,37 +166,45 @@ def tile_skeletonconv_t_kernel(tc, x, weight, dilation, step, grad_out, out):
                     in_=w_grouped[cc][:, k, :, :].rearrange("p c j -> p (c j)"),
                 )
 
-        def multiply(b, half):
+        def multiply(b, ct, half):
+            channels = slice(ct * C_TILE, (ct + 1) * C_TILE)
             columns = slice(b * POSITIONS + half * N_TILE, b * POSITIONS + (half + 1) * N_TILE)
-            for ct in range(C_TILES):
-                channels = slice(ct * C_TILE, (ct + 1) * C_TILE)
-                acc = psum.tile([C_TILE, N_TILE], F32)
-                for k in range(TAPS):
-                    nc.tensor.matmul_mx(
-                        out=acc[:],
-                        lhsT=w_codes[:, k, channels].bitcast(E4M3_X4),
-                        lhsT_scale=w_scales[:, k, channels],
-                        rhs=g_codes[k][:, columns].bitcast(E5M2_X4),
-                        rhs_scale=g_scales[k][:, columns],
-                        start=(k == 0),
-                        stop=(k == TAPS - 1),
-                    )
-                result = staging.tile([C_TILE, N_TILE], F32)
-                if ct % VECTOR_EMPTIES_EVERY == VECTOR_EMPTIES_EVERY - 1:
-                    nc.vector.tensor_copy(out=result[:], in_=acc[:])
-                else:
-                    nc.scalar.copy(out=result[:], in_=acc[:])
-                nc.sync.dma_start(
-                    out=out_rows[b, channels, half * N_TILE : (half + 1) * N_TILE], in_=result[:]
+            acc = psum.tile([C_TILE, N_TILE], F32)
+            for k in range(TAPS):
+                nc.tensor.matmul_mx(
+                    out=acc[:],
+                    lhsT=w_codes[:, k, channels].bitcast(E4M3_X4),
+                    lhsT_scale=w_scales[:, k, channels],
+                    rhs=g_codes[k][:, columns].bitcast(E5M2_X4),
+                    rhs_scale=g_scales[k][:, columns],
+                    start=(k == 0),
+                    stop=(k == TAPS - 1),
                 )
+            result = staging.tile([C_TILE, N_TILE], F32)
+            if b == BATCHES - 1 and half == 1:
+                nc.vector.tensor_copy(out=result[:], in_=acc[:])
+            else:
+                nc.scalar.copy(out=result[:], in_=acc[:])
+            nc.sync.dma_start(
+                out=out_rows[b, channels, half * N_TILE : (half + 1) * N_TILE], in_=result[:]
+            )
 
-        half_maps = [(b, half) for b in range(BATCHES) for half in range(HALVES)]
+        def prepare_map(b):
+            for half in range(HALVES):
+                prepare_grad(b, half)
+
         load_inputs()
+        wake_scalar()
         zero_outside_the_map()
-        prepare_grad(*half_maps[0])
-        for cc in range(C_CHUNKS):
+        prepare_grad(0, 0)
+        prepare_weight(0)
+        prepare_grad(0, 1)
+        for cc in range(1, C_CHUNKS):
             prepare_weight(cc)
-        for i in range(len(half_maps)):
-            if i + 1 < len(half_maps):
-                prepare_grad(*half_maps[i + 1])
-            multiply(*half_maps[i])
+        for b in range(BATCHES):
+            for cc in range(C_CHUNKS):
+                for half in range(HALVES):
+                    for ct in range(cc * C_CHUNK // C_TILE, (cc + 1) * C_CHUNK // C_TILE):
+                        multiply(b, ct, half)
+                if cc == 0 and b + 1 < BATCHES:
+                    prepare_map(b + 1)

@@ -50,7 +50,6 @@ def tile_skeletonconv_t_kernel(tc, x, weight, dilation, step, grad_out, out):
         keep = ctx.enter_context(tc.tile_pool(name="keep", bufs=1))
         staging = ctx.enter_context(tc.tile_pool(name="staging", bufs=STAGING_BUFS))
         psum = ctx.enter_context(tc.psum_pool(name="psum", bufs=PSUM_BANKS))
-        ctx.enter_context(tc.manual_schedule())
 
         g_raw = [
             [

@@ -5,6 +5,7 @@ import concourse.mybir as mybir
 BF16 = mybir.dt.bfloat16
 F32 = mybir.dt.float32
 U32 = mybir.dt.uint32
+I32 = mybir.dt.int32
 U8 = mybir.dt.uint8
 E4M3_X4 = mybir.dt.float8_e4m3fn_x4
 E5M2_X4 = mybir.dt.float8_e5m2_x4
@@ -13,6 +14,7 @@ P = 128
 PACK = 4
 BATCHES, C_IN, C_OUT, TAPS, HEIGHT, WIDTH = 2, 1024, 512, 3, 32, 32
 CENTRE = TAPS // 2
+TAP_ORDER = (1, 0, 2)
 POSITIONS = HEIGHT * WIDTH
 N_TILE = 512
 ROWS_TILE = N_TILE // WIDTH
@@ -61,10 +63,7 @@ def tile_skeletonconv_t_kernel(tc, x, weight, dilation, step, grad_out, out):
         w_raw = [
             keep.tile([P, PACK, C_CHUNK * TAPS], BF16, name="w_raw%d" % cc) for cc in range(C_CHUNKS)
         ]
-        g_tap = [
-            keep.tile([P, BATCHES, HEIGHT, WIDTH, PACK], BF16, name="g_tap%d" % k, align_bytes=64)
-            for k in range(TAPS)
-        ]
+        g_grouped = keep.tile([P, BATCHES, HEIGHT, WIDTH, PACK], BF16, align_bytes=64)
         g_codes = [
             keep.tile([P, BATCHES * POSITIONS], U32, name="g_codes%d" % k, align_bytes=64)
             for k in range(TAPS)
@@ -100,53 +99,63 @@ def tile_skeletonconv_t_kernel(tc, x, weight, dilation, step, grad_out, out):
             for b in range(1, BATCHES):
                 load_grad(b)
 
+        def as_map(plane):
+            return plane.rearrange("p (b h w) -> p b h w", b=BATCHES, h=HEIGHT)
+
         def zero_outside_the_map():
             for k in range(TAPS):
+                nc.vector.memset(g_scales[k][:].bitcast(I32), 0)
+                codes = as_map(g_codes[k][:].bitcast(I32))
                 row_lo, row_hi = inside(0, HEIGHT, (k - CENTRE) * step, HEIGHT)
                 col_lo, col_hi = inside(0, WIDTH, (k - CENTRE) * dilation, WIDTH)
                 for lo, hi in ((0, row_lo), (row_hi, HEIGHT)):
                     if lo < hi:
-                        nc.vector.memset(g_tap[k][:, :, lo:hi, :, :], 0.0)
+                        nc.vector.memset(codes[:, :, lo:hi, :], 0)
                 for lo, hi in ((0, col_lo), (col_hi, WIDTH)):
                     if lo < hi:
-                        nc.vector.memset(g_tap[k][:, :, :, lo:hi, :], 0.0)
+                        nc.vector.memset(codes[:, :, :, lo:hi], 0)
 
         def regroup_grad(b):
             for part, (first, end) in enumerate(row_parts):
                 engine_copy = nc.vector.tensor_copy if part == 0 else nc.scalar.copy
                 engine_copy(
-                    out=g_tap[CENTRE][:, b, first:end, :, :].rearrange(
+                    out=g_grouped[:, b, first:end, :, :].rearrange(
                         "p h (q i) j -> p (h q) j i", i=4
                     ),
                     in_=g_raw[b][part][:].rearrange("p j (q i) -> p q j i", i=4),
                 )
 
-        def quantise_grad(k, b, half):
-            rows = slice(half * ROWS_TILE, (half + 1) * ROWS_TILE)
-            columns = slice(b * POSITIONS + half * N_TILE, b * POSITIONS + (half + 1) * N_TILE)
+        def quantise_grad(b, first, end):
+            columns = slice(b * POSITIONS + first * WIDTH, b * POSITIONS + end * WIDTH)
             nc.vector.quantize_mx(
-                out=g_codes[k][:, columns].bitcast(E5M2_X4),
-                scales=g_scales[k][:, columns],
-                in_=g_tap[k][:, b, rows, :, :].rearrange("p h w j -> p (h w j)"),
+                out=g_codes[CENTRE][:, columns].bitcast(E5M2_X4),
+                scales=g_scales[CENTRE][:, columns],
+                in_=g_grouped[:, b, first:end, :, :].rearrange("p h w j -> p (h w j)"),
             )
 
         def shift_grad(k, b, half):
             down, right = (k - CENTRE) * step, (k - CENTRE) * dilation
             row_lo, row_hi = inside(half * ROWS_TILE, ROWS_TILE, down, HEIGHT)
             col_lo, col_hi = inside(0, WIDTH, right, WIDTH)
-            nc.vector.tensor_copy(
-                out=g_tap[k][:, b, row_lo:row_hi, col_lo:col_hi, :],
-                in_=g_tap[CENTRE][:, b, row_lo - down : row_hi - down, col_lo - right : col_hi - right, :],
-            )
+            for to, source in (
+                (as_map(g_codes[k][:].bitcast(I32)), as_map(g_codes[CENTRE][:].bitcast(I32))),
+                (as_map(g_scales[k][:]), as_map(g_scales[CENTRE][:])),
+            ):
+                nc.vector.tensor_copy(
+                    out=to[:, b, row_lo:row_hi, col_lo:col_hi],
+                    in_=source[:, b, row_lo - down : row_hi - down, col_lo - right : col_hi - right],
+                )
 
         def prepare_grad(b, half):
             if half == 0:
                 regroup_grad(b)
+                quantise_grad(b, 0, ROWS_TILE)
+                quantise_grad(b, ROWS_TILE, upper_rows)
+            else:
+                quantise_grad(b, ROWS_TILE, HEIGHT)
             for k in range(TAPS):
                 if k != CENTRE:
                     shift_grad(k, b, half)
-            for k in range(TAPS):
-                quantise_grad(k, b, half)
 
         def prepare_weight(cc):
             for engine_copy, cols in (
@@ -169,15 +178,15 @@ def tile_skeletonconv_t_kernel(tc, x, weight, dilation, step, grad_out, out):
             channels = slice(ct * C_TILE, (ct + 1) * C_TILE)
             columns = slice(b * POSITIONS + half * N_TILE, b * POSITIONS + (half + 1) * N_TILE)
             acc = psum.tile([C_TILE, N_TILE], F32)
-            for k in range(TAPS):
+            for k in TAP_ORDER:
                 nc.tensor.matmul_mx(
                     out=acc[:],
                     lhsT=w_codes[:, k, channels].bitcast(E4M3_X4),
                     lhsT_scale=w_scales[:, k, channels],
                     rhs=g_codes[k][:, columns].bitcast(E5M2_X4),
                     rhs_scale=g_scales[k][:, columns],
-                    start=(k == 0),
-                    stop=(k == TAPS - 1),
+                    start=(k == TAP_ORDER[0]),
+                    stop=(k == TAP_ORDER[-1]),
                 )
             result = staging.tile([C_TILE, N_TILE], F32)
             if b == BATCHES - 1 and half == 1:

@@ -23,7 +23,7 @@ C_TILE = P
 C_TILES = C_IN // C_TILE
 C_CHUNK = 2 * C_TILE
 C_CHUNKS = C_IN // C_CHUNK
-C_CHUNK_SCALAR = 5 * C_CHUNK // 8
+C_CHUNK_SCALAR = 3 * C_CHUNK // 8
 PSUM_BANKS = 8
 STAGING_BUFS = 6
 

@@ -21,11 +21,11 @@ ROWS_TILE = N_TILE // WIDTH
 HALVES = POSITIONS // N_TILE
 C_TILE = P
 C_TILES = C_IN // C_TILE
-C_CHUNK = 2 * C_TILE
-C_CHUNKS = C_IN // C_CHUNK
-C_CHUNK_SCALAR = 3 * C_CHUNK // 8
+W_CHUNKS = ((0, 1), (1, 1), (2, 2), (4, 2), (6, 2))
+W_SCALAR_EIGHTHS = (5, 5, 5, 4, 4)
 PSUM_BANKS = 8
 STAGING_BUFS = 6
+EMPTY_LAG = 3
 
 FLOPS = 2 * BATCHES * C_IN * POSITIONS * C_OUT * TAPS
 BYTES = 2 * C_OUT * C_IN * TAPS + 2 * BATCHES * C_OUT * POSITIONS + 4 * BATCHES * C_IN * POSITIONS
@@ -43,6 +43,7 @@ def tile_skeletonconv_t_kernel(tc, x, weight, dilation, step, grad_out, out):
 
     upper_rows = ROWS_TILE + CENTRE * step
     row_parts = ((0, upper_rows), (upper_rows, HEIGHT))
+    vector_rows = (11, 8)
 
     grad_rows = grad_out.rearrange("b (p j) h w -> b p j (h w)", j=PACK)
     weight_rows = weight.rearrange("(p j) c k -> p j (c k)", j=PACK)
@@ -52,6 +53,7 @@ def tile_skeletonconv_t_kernel(tc, x, weight, dilation, step, grad_out, out):
         keep = ctx.enter_context(tc.tile_pool(name="keep", bufs=1))
         staging = ctx.enter_context(tc.tile_pool(name="staging", bufs=STAGING_BUFS))
         psum = ctx.enter_context(tc.psum_pool(name="psum", bufs=PSUM_BANKS))
+        ctx.enter_context(tc.manual_schedule())
 
         g_raw = [
             [
@@ -61,7 +63,8 @@ def tile_skeletonconv_t_kernel(tc, x, weight, dilation, step, grad_out, out):
             for b in range(BATCHES)
         ]
         w_raw = [
-            keep.tile([P, PACK, C_CHUNK * TAPS], BF16, name="w_raw%d" % cc) for cc in range(C_CHUNKS)
+            keep.tile([P, PACK, count * C_TILE * TAPS], BF16, name="w_raw%d" % first)
+            for first, count in W_CHUNKS
         ]
         g_grouped = keep.tile([P, BATCHES, HEIGHT, WIDTH, PACK], BF16, align_bytes=64)
         g_codes = [
@@ -73,8 +76,8 @@ def tile_skeletonconv_t_kernel(tc, x, weight, dilation, step, grad_out, out):
             for k in range(TAPS)
         ]
         w_grouped = [
-            keep.tile([P, TAPS, C_CHUNK, PACK], BF16, name="w_grouped%d" % cc, align_bytes=64)
-            for cc in range(C_CHUNKS)
+            keep.tile([P, TAPS, count * C_TILE, PACK], BF16, name="w_grouped%d" % first, align_bytes=64)
+            for first, count in W_CHUNKS
         ]
         w_codes = keep.tile([P, TAPS, C_IN], U32, align_bytes=64)
         w_scales = keep.tile([P, TAPS, C_IN], U8, align_bytes=64)
@@ -85,19 +88,16 @@ def tile_skeletonconv_t_kernel(tc, x, weight, dilation, step, grad_out, out):
             nc.vector.memset(column[:], 0.0)
             nc.scalar.copy(out=column_copy[:], in_=column[:])
 
-        def load_grad(b):
-            for part, (first, end) in enumerate(row_parts):
-                nc.sync.dma_start(
-                    out=g_raw[b][part][:], in_=grad_rows[b][:, :, first * WIDTH : end * WIDTH]
-                )
+        def load_grad(b, part):
+            first, end = row_parts[part]
+            nc.sync.dma_start(
+                out=g_raw[b][part][:], in_=grad_rows[b][:, :, first * WIDTH : end * WIDTH]
+            )
 
-        def load_inputs():
-            load_grad(0)
-            for cc in range(C_CHUNKS):
-                columns = slice(cc * C_CHUNK * TAPS, (cc + 1) * C_CHUNK * TAPS)
-                nc.sync.dma_start(out=w_raw[cc][:], in_=weight_rows[:, :, columns])
-            for b in range(1, BATCHES):
-                load_grad(b)
+        def load_weight(i):
+            first, count = W_CHUNKS[i]
+            columns = slice(first * C_TILE * TAPS, (first + count) * C_TILE * TAPS)
+            nc.sync.dma_start(out=w_raw[i][:], in_=weight_rows[:, :, columns])
 
         def as_map(plane):
             return plane.rearrange("p (b h w) -> p b h w", b=BATCHES, h=HEIGHT)
@@ -115,15 +115,23 @@ def tile_skeletonconv_t_kernel(tc, x, weight, dilation, step, grad_out, out):
                     if lo < hi:
                         nc.vector.memset(codes[:, :, :, lo:hi], 0)
 
-        def regroup_grad(b):
-            for part, (first, end) in enumerate(row_parts):
-                engine_copy = nc.vector.tensor_copy if part == 0 else nc.scalar.copy
-                engine_copy(
-                    out=g_grouped[:, b, first:end, :, :].rearrange(
-                        "p h (q i) j -> p (h q) j i", i=4
-                    ),
-                    in_=g_raw[b][part][:].rearrange("p j (q i) -> p q j i", i=4),
-                )
+        def regroup_grad(engine_copy, b, part, lo, hi):
+            first = row_parts[part][0]
+            engine_copy(
+                out=g_grouped[:, b, first + lo : first + hi, :, :].rearrange(
+                    "p h (q i) j -> p (h q) j i", i=4
+                ),
+                in_=g_raw[b][part][:, :, lo * WIDTH : hi * WIDTH].rearrange(
+                    "p j (q i) -> p q j i", i=4
+                ),
+            )
+
+        def regroup_grad_vector(b, part):
+            regroup_grad(nc.vector.tensor_copy, b, part, 0, vector_rows[part])
+
+        def regroup_grad_scalar(b, part):
+            first, end = row_parts[part]
+            regroup_grad(nc.scalar.copy, b, part, vector_rows[part], end - first)
 
         def quantise_grad(b, first, end):
             columns = slice(b * POSITIONS + first * WIDTH, b * POSITIONS + end * WIDTH)
@@ -133,46 +141,69 @@ def tile_skeletonconv_t_kernel(tc, x, weight, dilation, step, grad_out, out):
                 in_=g_grouped[:, b, first:end, :, :].rearrange("p h w j -> p (h w j)"),
             )
 
-        def shift_grad(k, b, half):
-            down, right = (k - CENTRE) * step, (k - CENTRE) * dilation
-            row_lo, row_hi = inside(half * ROWS_TILE, ROWS_TILE, down, HEIGHT)
-            col_lo, col_hi = inside(0, WIDTH, right, WIDTH)
-            for to, source in (
-                (as_map(g_codes[k][:].bitcast(I32)), as_map(g_codes[CENTRE][:].bitcast(I32))),
-                (as_map(g_scales[k][:]), as_map(g_scales[CENTRE][:])),
-            ):
-                nc.vector.tensor_copy(
-                    out=to[:, b, row_lo:row_hi, col_lo:col_hi],
-                    in_=source[:, b, row_lo - down : row_hi - down, col_lo - right : col_hi - right],
-                )
-
-        def prepare_grad(b, half):
+        def quantise_half(b, half):
             if half == 0:
-                regroup_grad(b)
                 quantise_grad(b, 0, ROWS_TILE)
                 quantise_grad(b, ROWS_TILE, upper_rows)
             else:
                 quantise_grad(b, ROWS_TILE, HEIGHT)
-            for k in range(TAPS):
-                if k != CENTRE:
-                    shift_grad(k, b, half)
 
-        def prepare_weight(cc):
-            for engine_copy, cols in (
-                (nc.scalar.copy, slice(0, C_CHUNK_SCALAR)),
-                (nc.vector.tensor_copy, slice(C_CHUNK_SCALAR, C_CHUNK)),
-            ):
-                engine_copy(
-                    out=w_grouped[cc][:, :, cols, :].rearrange("p k c j -> p c j k"),
-                    in_=w_raw[cc][:].rearrange("p j (c k) -> p c j k", k=TAPS)[:, cols, :, :],
-                )
-            columns = slice(cc * C_CHUNK, (cc + 1) * C_CHUNK)
-            for k in range(TAPS):
+        def shift_grad(b, half):
+            for k in TAP_ORDER[1:]:
+                down, right = (k - CENTRE) * step, (k - CENTRE) * dilation
+                row_lo, row_hi = inside(half * ROWS_TILE, ROWS_TILE, down, HEIGHT)
+                col_lo, col_hi = inside(0, WIDTH, right, WIDTH)
+                for to, source in (
+                    (as_map(g_codes[k][:].bitcast(I32)), as_map(g_codes[CENTRE][:].bitcast(I32))),
+                    (as_map(g_scales[k][:]), as_map(g_scales[CENTRE][:])),
+                ):
+                    nc.vector.tensor_copy(
+                        out=to[:, b, row_lo:row_hi, col_lo:col_hi],
+                        in_=source[
+                            :, b, row_lo - down : row_hi - down, col_lo - right : col_hi - right
+                        ],
+                    )
+
+        def regroup_weight(engine_copy, i, cols):
+            engine_copy(
+                out=w_grouped[i][:, :, cols, :].rearrange("p k c j -> p c j k"),
+                in_=w_raw[i][:].rearrange("p j (c k) -> p c j k", k=TAPS)[:, cols, :, :],
+            )
+
+        def scalar_columns(i):
+            return W_CHUNKS[i][1] * C_TILE * W_SCALAR_EIGHTHS[i] // 8
+
+        def regroup_weight_scalar(i):
+            regroup_weight(nc.scalar.copy, i, slice(0, scalar_columns(i)))
+
+        def regroup_weight_vector(i):
+            regroup_weight(nc.vector.tensor_copy, i, slice(scalar_columns(i), W_CHUNKS[i][1] * C_TILE))
+
+        def quantise_weight(i):
+            first, count = W_CHUNKS[i]
+            columns = slice(first * C_TILE, (first + count) * C_TILE)
+            for k in TAP_ORDER:
                 nc.vector.quantize_mx(
                     out=w_codes[:, k, columns].bitcast(E4M3_X4),
                     scales=w_scales[:, k, columns],
-                    in_=w_grouped[cc][:, k, :, :].rearrange("p c j -> p (c j)"),
+                    in_=w_grouped[i][:, k, :, :].rearrange("p c j -> p (c j)"),
                 )
+
+        multiplied = []
+        emptied = []
+
+        def empty_oldest():
+            acc, b, ct, half = multiplied[len(emptied)]
+            result = staging.tile([C_TILE, N_TILE], F32)
+            if b == BATCHES - 1 and len(emptied) % 2 == 1:
+                nc.vector.tensor_copy(out=result[:], in_=acc[:])
+            else:
+                nc.scalar.copy(out=result[:], in_=acc[:])
+            emptied.append(ct)
+            nc.sync.dma_start(
+                out=out_rows[b, ct * C_TILE : (ct + 1) * C_TILE, half * N_TILE : (half + 1) * N_TILE],
+                in_=result[:],
+            )
 
         def multiply(b, ct, half):
             channels = slice(ct * C_TILE, (ct + 1) * C_TILE)
@@ -188,31 +219,55 @@ def tile_skeletonconv_t_kernel(tc, x, weight, dilation, step, grad_out, out):
                     start=(k == TAP_ORDER[0]),
                     stop=(k == TAP_ORDER[-1]),
                 )
-            result = staging.tile([C_TILE, N_TILE], F32)
-            if b == BATCHES - 1 and half == 1:
-                nc.vector.tensor_copy(out=result[:], in_=acc[:])
-            else:
-                nc.scalar.copy(out=result[:], in_=acc[:])
-            nc.sync.dma_start(
-                out=out_rows[b, channels, half * N_TILE : (half + 1) * N_TILE], in_=result[:]
-            )
+            multiplied.append((acc, b, ct, half))
+            while len(multiplied) - len(emptied) > EMPTY_LAG:
+                empty_oldest()
 
-        def prepare_map(b):
-            for half in range(HALVES):
-                prepare_grad(b, half)
-
-        load_inputs()
+        load_grad(0, 0)
+        load_weight(0)
+        load_weight(1)
+        load_grad(0, 1)
+        for i in range(2, len(W_CHUNKS)):
+            load_weight(i)
+        for part in range(len(row_parts)):
+            load_grad(1, part)
         wake_scalar()
         zero_outside_the_map()
-        prepare_grad(0, 0)
-        prepare_weight(0)
-        prepare_grad(0, 1)
-        for cc in range(1, C_CHUNKS):
-            prepare_weight(cc)
-        for b in range(BATCHES):
-            for cc in range(C_CHUNKS):
+
+        regroup_grad_vector(0, 0)
+        regroup_grad_scalar(0, 0)
+        regroup_weight_scalar(0)
+        regroup_weight_vector(0)
+        quantise_half(0, 0)
+        quantise_weight(0)
+        shift_grad(0, 0)
+        regroup_weight_scalar(1)
+        regroup_grad_scalar(0, 1)
+        regroup_weight_vector(1)
+        regroup_grad_vector(0, 1)
+        quantise_weight(1)
+        quantise_half(0, 1)
+        shift_grad(0, 1)
+        for half in range(HALVES):
+            for ct in range(2):
+                multiply(0, ct, half)
+        for i in range(2, len(W_CHUNKS)):
+            regroup_weight_scalar(i)
+            regroup_weight_vector(i)
+            quantise_weight(i)
+        for i in range(2, len(W_CHUNKS)):
+            first, count = W_CHUNKS[i]
+            for half in range(HALVES):
+                for ct in range(first, first + count):
+                    multiply(0, ct, half)
+            if i == 2:
                 for half in range(HALVES):
-                    for ct in range(cc * C_CHUNK // C_TILE, (cc + 1) * C_CHUNK // C_TILE):
-                        multiply(b, ct, half)
-                if cc == 0 and b + 1 < BATCHES:
-                    prepare_map(b + 1)
+                    regroup_grad_scalar(1, half)
+                    regroup_grad_vector(1, half)
+                    quantise_half(1, half)
+                    shift_grad(1, half)
+        for half in range(HALVES):
+            for ct in range(C_TILES):
+                multiply(1, ct, half)
+        while len(emptied) < len(multiplied):
+            empty_oldest()

@@ -26,6 +26,8 @@ W_SCALAR_EIGHTHS = (5, 5, 5, 4, 4)
 PSUM_BANKS = 8
 STAGING_BUFS = 6
 EMPTY_LAG = 3
+LAST_PIECES = 2
+WARM_FREE, WARM_LOADED = 8, 4
 
 FLOPS = 2 * BATCHES * C_IN * POSITIONS * C_OUT * TAPS
 BYTES = 2 * C_OUT * C_IN * TAPS + 2 * BATCHES * C_OUT * POSITIONS + 4 * BATCHES * C_IN * POSITIONS
@@ -87,6 +89,18 @@ def tile_skeletonconv_t_kernel(tc, x, weight, dilation, step, grad_out, out):
             column_copy = keep.tile([P, 1], F32)
             nc.vector.memset(column[:], 0.0)
             nc.scalar.copy(out=column_copy[:], in_=column[:])
+
+        def warm_up():
+            zeros = keep.tile([P, N_TILE], BF16)
+            nc.vector.memset(zeros[:], 0.0)
+            acc = psum.tile([C_TILE, N_TILE], F32)
+            moving = [zeros[:]] * WARM_FREE
+            moving += [g_raw[0][0][:, 0, :N_TILE]] * WARM_LOADED
+            moving += [w_raw[0][:, 0, :]] * WARM_LOADED
+            for rhs in moving:
+                nc.tensor.matmul(
+                    out=acc[:, : rhs.shape[1]], lhsT=zeros[:, :P], rhs=rhs, start=True, stop=True
+                )
 
         def load_grad(b, part):
             first, end = row_parts[part]
@@ -196,14 +210,23 @@ def tile_skeletonconv_t_kernel(tc, x, weight, dilation, step, grad_out, out):
             acc, b, ct, half = multiplied[len(emptied)]
             result = staging.tile([C_TILE, N_TILE], F32)
             if b == BATCHES - 1 and len(emptied) % 2 == 1:
-                nc.vector.tensor_copy(out=result[:], in_=acc[:])
+                engine_copy = nc.vector.tensor_copy
             else:
-                nc.scalar.copy(out=result[:], in_=acc[:])
+                engine_copy = nc.scalar.copy
             emptied.append(ct)
-            nc.sync.dma_start(
-                out=out_rows[b, ct * C_TILE : (ct + 1) * C_TILE, half * N_TILE : (half + 1) * N_TILE],
-                in_=result[:],
-            )
+            pieces = LAST_PIECES if len(emptied) == BATCHES * C_TILES * HALVES else 1
+            width = N_TILE // pieces
+            for piece in range(pieces):
+                cols = slice(piece * width, (piece + 1) * width)
+                engine_copy(out=result[:, cols], in_=acc[:, cols])
+                nc.sync.dma_start(
+                    out=out_rows[
+                        b,
+                        ct * C_TILE : (ct + 1) * C_TILE,
+                        half * N_TILE + piece * width : half * N_TILE + (piece + 1) * width,
+                    ],
+                    in_=result[:, cols],
+                )
 
         def multiply(b, ct, half):
             channels = slice(ct * C_TILE, (ct + 1) * C_TILE)
@@ -232,6 +255,7 @@ def tile_skeletonconv_t_kernel(tc, x, weight, dilation, step, grad_out, out):
         for part in range(len(row_parts)):
             load_grad(1, part)
         wake_scalar()
+        warm_up()
         zero_outside_the_map()
 
         regroup_grad_vector(0, 0)

@@ -180,8 +180,10 @@ def tile_skeletonconv_t_kernel(tc, x, weight, dilation, step, grad_out, out):
 
         def regroup_weight(engine_copy, i, cols):
             engine_copy(
-                out=w_grouped[i][:, :, cols, :].rearrange("p k c j -> p c j k"),
-                in_=w_raw[i][:].rearrange("p j (c k) -> p c j k", k=TAPS)[:, cols, :, :],
+                out=w_grouped[i][:, :, cols, :].rearrange("p k (c e) j -> p c j e k", e=2),
+                in_=w_raw[i][:].rearrange("p j (c k) -> p j c k", k=TAPS)[:, :, cols, :].rearrange(
+                    "p j (c e) k -> p c j e k", e=2
+                ),
             )
 
         def scalar_columns(i):

@@ -21,11 +21,12 @@ ROWS_TILE = N_TILE // WIDTH
 HALVES = POSITIONS // N_TILE
 C_TILE = P
 C_TILES = C_IN // C_TILE
-W_CHUNKS = ((0, 1), (1, 1), (2, 2), (4, 2), (6, 2))
-W_SCALAR_EIGHTHS = (5, 5, 5, 4, 4)
+W_CHUNKS = ((0, 1), (1, 1), (2, 1), (3, 1), (4, 2), (6, 2))
+W_SCALAR_EIGHTHS = (5, 5, 5, 5, 4, 4)
 PSUM_BANKS = 8
 STAGING_BUFS = 6
 EMPTY_LAG = 3
+WEIGHTS_AHEAD = 2
 LAST_PIECES = 2
 WARM_FREE, WARM_LOADED = 8, 4
 
@@ -230,23 +231,25 @@ def tile_skeletonconv_t_kernel(tc, x, weight, dilation, step, grad_out, out):
                     in_=result[:, cols],
                 )
 
-        def multiply(b, ct, half):
-            channels = slice(ct * C_TILE, (ct + 1) * C_TILE)
+        def multiply(b, channel_tiles, half):
             columns = slice(b * POSITIONS + half * N_TILE, b * POSITIONS + (half + 1) * N_TILE)
-            acc = psum.tile([C_TILE, N_TILE], F32)
+            accs = [psum.tile([C_TILE, N_TILE], F32, name="acc") for ct in channel_tiles]
             for k in TAP_ORDER:
-                nc.tensor.matmul_mx(
-                    out=acc[:],
-                    lhsT=w_codes[:, k, channels].bitcast(E4M3_X4),
-                    lhsT_scale=w_scales[:, k, channels],
-                    rhs=g_codes[k][:, columns].bitcast(E5M2_X4),
-                    rhs_scale=g_scales[k][:, columns],
-                    start=(k == TAP_ORDER[0]),
-                    stop=(k == TAP_ORDER[-1]),
-                )
-            multiplied.append((acc, b, ct, half))
-            while len(multiplied) - len(emptied) > EMPTY_LAG:
-                empty_oldest()
+                for acc, ct in zip(accs, channel_tiles):
+                    channels = slice(ct * C_TILE, (ct + 1) * C_TILE)
+                    nc.tensor.matmul_mx(
+                        out=acc[:],
+                        lhsT=w_codes[:, k, channels].bitcast(E4M3_X4),
+                        lhsT_scale=w_scales[:, k, channels],
+                        rhs=g_codes[k][:, columns].bitcast(E5M2_X4),
+                        rhs_scale=g_scales[k][:, columns],
+                        start=(k == TAP_ORDER[0]),
+                        stop=(k == TAP_ORDER[-1]),
+                    )
+            for acc, ct in zip(accs, channel_tiles):
+                multiplied.append((acc, b, ct, half))
+                while len(multiplied) - len(emptied) > EMPTY_LAG:
+                    empty_oldest()
 
         load_grad(0, 0)
         load_weight(0)
@@ -274,19 +277,24 @@ def tile_skeletonconv_t_kernel(tc, x, weight, dilation, step, grad_out, out):
         quantise_weight(1)
         quantise_half(0, 1)
         shift_grad(0, 1)
-        for half in range(HALVES):
-            for ct in range(2):
-                multiply(0, ct, half)
-        for i in range(2, len(W_CHUNKS)):
+        def prepare_weight(i):
             regroup_weight_scalar(i)
             regroup_weight_vector(i)
             quantise_weight(i)
+
+        for i in range(2, 2 + WEIGHTS_AHEAD):
+            prepare_weight(i)
+        multiply(0, (0,), 0)
+        multiply(0, (1,), 0)
+        multiply(0, (0, 1), 1)
         for i in range(2, len(W_CHUNKS)):
+            if i + WEIGHTS_AHEAD < len(W_CHUNKS):
+                prepare_weight(i + WEIGHTS_AHEAD)
             first, count = W_CHUNKS[i]
             for half in range(HALVES):
                 for ct in range(first, first + count):
-                    multiply(0, ct, half)
-            if i == 2:
+                    multiply(0, (ct,), half)
+            if i == 3:
                 for half in range(HALVES):
                     regroup_grad_scalar(1, half)
                     regroup_grad_vector(1, half)
@@ -294,6 +302,6 @@ def tile_skeletonconv_t_kernel(tc, x, weight, dilation, step, grad_out, out):
                     shift_grad(1, half)
         for half in range(HALVES):
             for ct in range(C_TILES):
-                multiply(1, ct, half)
+                multiply(1, (ct,), half)
         while len(emptied) < len(multiplied):
             empty_oldest()

@@ -24,7 +24,7 @@ C_TILES = C_IN // C_TILE
 W_CHUNKS = ((0, 1), (1, 1), (2, 1), (3, 1), (4, 2), (6, 2))
 W_SCALAR_EIGHTHS = (5, 5, 5, 5, 4, 4)
 PSUM_BANKS = 8
-STAGING_BUFS = 6
+STAGING_BUFS = BATCHES * C_TILES
 EMPTY_LAG = 3
 WEIGHTS_AHEAD = 2
 LAST_PIECES = 2
@@ -208,28 +208,31 @@ def tile_skeletonconv_t_kernel(tc, x, weight, dilation, step, grad_out, out):
 
         multiplied = []
         emptied = []
+        results = {}
 
         def empty_oldest():
             acc, b, ct, half = multiplied[len(emptied)]
-            result = staging.tile([C_TILE, N_TILE], F32)
+            if (b, ct) not in results:
+                results[(b, ct)] = [staging.tile([C_TILE, POSITIONS], F32, name="result"), 0]
+            result = results[(b, ct)][0]
+            results[(b, ct)][1] += 1
             if b == BATCHES - 1 and len(emptied) % 2 == 1:
                 engine_copy = nc.vector.tensor_copy
             else:
                 engine_copy = nc.scalar.copy
             emptied.append(ct)
+            channels = slice(ct * C_TILE, (ct + 1) * C_TILE)
+            if (b, ct) != (BATCHES - 1, C_TILES - 1):
+                engine_copy(out=result[:, half * N_TILE : (half + 1) * N_TILE], in_=acc[:])
+                if results[(b, ct)][1] == HALVES:
+                    nc.sync.dma_start(out=out_rows[b, channels, :], in_=result[:])
+                return
             pieces = LAST_PIECES if len(emptied) == BATCHES * C_TILES * HALVES else 1
             width = N_TILE // pieces
             for piece in range(pieces):
-                cols = slice(piece * width, (piece + 1) * width)
-                engine_copy(out=result[:, cols], in_=acc[:, cols])
-                nc.sync.dma_start(
-                    out=out_rows[
-                        b,
-                        ct * C_TILE : (ct + 1) * C_TILE,
-                        half * N_TILE + piece * width : half * N_TILE + (piece + 1) * width,
-                    ],
-                    in_=result[:, cols],
-                )
+                cols = slice(half * N_TILE + piece * width, half * N_TILE + (piece + 1) * width)
+                engine_copy(out=result[:, cols], in_=acc[:, piece * width : (piece + 1) * width])
+                nc.sync.dma_start(out=out_rows[b, channels, cols], in_=result[:, cols])
 
         def multiply(b, channel_tiles, half):
             columns = slice(b * POSITIONS + half * N_TILE, b * POSITIONS + (half + 1) * N_TILE)
@@ -301,7 +304,10 @@ def tile_skeletonconv_t_kernel(tc, x, weight, dilation, step, grad_out, out):
                     quantise_half(1, half)
                     shift_grad(1, half)
         for half in range(HALVES):
-            for ct in range(C_TILES):
+            for ct in range(2):
+                multiply(1, (ct,), half)
+        for ct in range(2, C_TILES):
+            for half in range(HALVES):
                 multiply(1, (ct,), half)
         while len(emptied) < len(multiplied):
             empty_oldest()

@@ -22,7 +22,7 @@ HALVES = POSITIONS // N_TILE
 C_TILE = P
 C_TILES = C_IN // C_TILE
 W_CHUNKS = ((0, 1), (1, 1), (2, 1), (3, 1), (4, 2), (6, 2))
-W_SCALAR_EIGHTHS = (5, 5, 5, 5, 4, 4)
+W_SCALAR_EIGHTHS = (5, 7, 7, 5, 3, 3)
 PSUM_BANKS = 8
 STAGING_BUFS = BATCHES * C_TILES
 EMPTY_LAG = 3
@@ -46,7 +46,7 @@ def tile_skeletonconv_t_kernel(tc, x, weight, dilation, step, grad_out, out):
 
     upper_rows = ROWS_TILE + CENTRE * step
     row_parts = ((0, upper_rows), (upper_rows, HEIGHT))
-    vector_rows = (11, 8)
+    vector_rows = ((11, 6), (11, 8))
 
     grad_rows = grad_out.rearrange("b (p j) h w -> b p j (h w)", j=PACK)
     weight_rows = weight.rearrange("(p j) c k -> p j (c k)", j=PACK)
@@ -142,11 +142,11 @@ def tile_skeletonconv_t_kernel(tc, x, weight, dilation, step, grad_out, out):
             )
 
         def regroup_grad_vector(b, part):
-            regroup_grad(nc.vector.tensor_copy, b, part, 0, vector_rows[part])
+            regroup_grad(nc.vector.tensor_copy, b, part, 0, vector_rows[b][part])
 
         def regroup_grad_scalar(b, part):
             first, end = row_parts[part]
-            regroup_grad(nc.scalar.copy, b, part, vector_rows[part], end - first)
+            regroup_grad(nc.scalar.copy, b, part, vector_rows[b][part], end - first)
 
         def quantise_grad(b, first, end):
             columns = slice(b * POSITIONS + first * WIDTH, b * POSITIONS + end * WIDTH)
@@ -279,13 +279,16 @@ def tile_skeletonconv_t_kernel(tc, x, weight, dilation, step, grad_out, out):
         regroup_grad_vector(0, 1)
         quantise_weight(1)
         quantise_half(0, 1)
+        regroup_weight_scalar(2)
+        regroup_weight_vector(2)
         shift_grad(0, 1)
+        quantise_weight(2)
         def prepare_weight(i):
             regroup_weight_scalar(i)
             regroup_weight_vector(i)
             quantise_weight(i)
 
-        for i in range(2, 2 + WEIGHTS_AHEAD):
+        for i in range(3, 2 + WEIGHTS_AHEAD):
             prepare_weight(i)
         multiply(0, (0,), 0)
         multiply(0, (1,), 0)

@@ -134,10 +134,10 @@ def tile_skeletonconv_t_kernel(tc, x, weight, dilation, step, grad_out, out):
             first = row_parts[part][0]
             engine_copy(
                 out=g_grouped[:, b, first + lo : first + hi, :, :].rearrange(
-                    "p h (q i) j -> p (h q) j i", i=4
+                    "p h (q i) j -> p (h q) j i", i=8
                 ),
                 in_=g_raw[b][part][:, :, lo * WIDTH : hi * WIDTH].rearrange(
-                    "p j (q i) -> p q j i", i=4
+                    "p j (q i) -> p q j i", i=8
                 ),
             )
 

from contextlib import ExitStack

import concourse.mybir as mybir

BF16 = mybir.dt.bfloat16
F32 = mybir.dt.float32
U32 = mybir.dt.uint32
I32 = mybir.dt.int32
U8 = mybir.dt.uint8
E4M3_X4 = mybir.dt.float8_e4m3fn_x4
E5M2_X4 = mybir.dt.float8_e5m2_x4

P = 128
PACK = 4
BATCHES, C_IN, C_OUT, TAPS, HEIGHT, WIDTH = 2, 1024, 512, 3, 32, 32
CENTRE = TAPS // 2
TAP_ORDER = (1, 0, 2)
POSITIONS = HEIGHT * WIDTH
N_TILE = 512
ROWS_TILE = N_TILE // WIDTH
HALVES = POSITIONS // N_TILE
C_TILE = P
C_TILES = C_IN // C_TILE
W_CHUNKS = ((0, 1), (1, 1), (2, 1), (3, 1), (4, 2), (6, 2))
W_SCALAR_EIGHTHS = (5, 7, 7, 5, 3, 3)
PSUM_BANKS = 8
STAGING_BUFS = BATCHES * C_TILES
EMPTY_LAG = 3
WEIGHTS_AHEAD = 2
LAST_PIECES = 2
WARM_FREE, WARM_LOADED = 8, 4

FLOPS = 2 * BATCHES * C_IN * POSITIONS * C_OUT * TAPS
BYTES = 2 * C_OUT * C_IN * TAPS + 2 * BATCHES * C_OUT * POSITIONS + 4 * BATCHES * C_IN * POSITIONS


def inside(first, count, shift, size):
    return max(first, shift), min(first + count, size + shift)


def tile_skeletonconv_t_kernel(tc, x, weight, dilation, step, grad_out, out):
    nc = tc.nc
    assert tuple(grad_out.shape) == (BATCHES, C_OUT, HEIGHT, WIDTH)
    assert tuple(weight.shape) == (C_OUT, C_IN, TAPS)
    assert C_OUT == P * PACK

    upper_rows = ROWS_TILE + CENTRE * step
    row_parts = ((0, upper_rows), (upper_rows, HEIGHT))
    vector_rows = ((11, 6), (11, 8))

    grad_rows = grad_out.rearrange("b (p j) h w -> b p j (h w)", j=PACK)
    weight_rows = weight.rearrange("(p j) c k -> p j (c k)", j=PACK)
    out_rows = out.rearrange("b c h w -> b c (h w)")

    with ExitStack() as ctx:
        keep = ctx.enter_context(tc.tile_pool(name="keep", bufs=1))
        staging = ctx.enter_context(tc.tile_pool(name="staging", bufs=STAGING_BUFS))
        psum = ctx.enter_context(tc.psum_pool(name="psum", bufs=PSUM_BANKS))
        ctx.enter_context(tc.manual_schedule())

        g_raw = [
            [
                keep.tile([P, PACK, (end - first) * WIDTH], BF16, name="g_raw%d_%d" % (b, first))
                for first, end in row_parts
            ]
            for b in range(BATCHES)
        ]
        w_raw = [
            keep.tile([P, PACK, count * C_TILE * TAPS], BF16, name="w_raw%d" % first)
            for first, count in W_CHUNKS
        ]
        g_grouped = keep.tile([P, BATCHES, HEIGHT, WIDTH, PACK], BF16, align_bytes=64)
        g_codes = [
            keep.tile([P, BATCHES * POSITIONS], U32, name="g_codes%d" % k, align_bytes=64)
            for k in range(TAPS)
        ]
        g_scales = [
            keep.tile([P, BATCHES * POSITIONS], U8, name="g_scales%d" % k, align_bytes=64)
            for k in range(TAPS)
        ]
        w_grouped = [
            keep.tile([P, TAPS, count * C_TILE, PACK], BF16, name="w_grouped%d" % first, align_bytes=64)
            for first, count in W_CHUNKS
        ]
        w_codes = keep.tile([P, TAPS, C_IN], U32, align_bytes=64)
        w_scales = keep.tile([P, TAPS, C_IN], U8, align_bytes=64)

        def wake_scalar():
            column = keep.tile([P, 1], F32)
            column_copy = keep.tile([P, 1], F32)
            nc.vector.memset(column[:], 0.0)
            nc.scalar.copy(out=column_copy[:], in_=column[:])

        def warm_up():
            zeros = keep.tile([P, N_TILE], BF16)
            nc.vector.memset(zeros[:], 0.0)
            acc = psum.tile([C_TILE, N_TILE], F32)
            moving = [zeros[:]] * WARM_FREE
            moving += [g_raw[0][0][:, 0, :N_TILE]] * WARM_LOADED
            moving += [w_raw[0][:, 0, :]] * WARM_LOADED
            for rhs in moving:
                nc.tensor.matmul(
                    out=acc[:, : rhs.shape[1]], lhsT=zeros[:, :P], rhs=rhs, start=True, stop=True
                )

        def load_grad(b, part):
            first, end = row_parts[part]
            nc.sync.dma_start(
                out=g_raw[b][part][:], in_=grad_rows[b][:, :, first * WIDTH : end * WIDTH]
            )

        def load_weight(i):
            first, count = W_CHUNKS[i]
            columns = slice(first * C_TILE * TAPS, (first + count) * C_TILE * TAPS)
            nc.sync.dma_start(out=w_raw[i][:], in_=weight_rows[:, :, columns])

        def as_map(plane):
            return plane.rearrange("p (b h w) -> p b h w", b=BATCHES, h=HEIGHT)

        def zero_outside_the_map():
            for k in range(TAPS):
                nc.vector.memset(g_scales[k][:].bitcast(I32), 0)
                codes = as_map(g_codes[k][:].bitcast(I32))
                row_lo, row_hi = inside(0, HEIGHT, (k - CENTRE) * step, HEIGHT)
                col_lo, col_hi = inside(0, WIDTH, (k - CENTRE) * dilation, WIDTH)
                for lo, hi in ((0, row_lo), (row_hi, HEIGHT)):
                    if lo < hi:
                        nc.vector.memset(codes[:, :, lo:hi, :], 0)
                for lo, hi in ((0, col_lo), (col_hi, WIDTH)):
                    if lo < hi:
                        nc.vector.memset(codes[:, :, :, lo:hi], 0)

        def regroup_grad(engine_copy, b, part, lo, hi):
            first = row_parts[part][0]
            engine_copy(
                out=g_grouped[:, b, first + lo : first + hi, :, :].rearrange(
                    "p h (q i) j -> p (h q) j i", i=8
                ),
                in_=g_raw[b][part][:, :, lo * WIDTH : hi * WIDTH].rearrange(
                    "p j (q i) -> p q j i", i=8
                ),
            )

        def regroup_grad_vector(b, part):
            regroup_grad(nc.vector.tensor_copy, b, part, 0, vector_rows[b][part])

        def regroup_grad_scalar(b, part):
            first, end = row_parts[part]
            regroup_grad(nc.scalar.copy, b, part, vector_rows[b][part], end - first)

        def quantise_grad(b, first, end):
            columns = slice(b * POSITIONS + first * WIDTH, b * POSITIONS + end * WIDTH)
            nc.vector.quantize_mx(
                out=g_codes[CENTRE][:, columns].bitcast(E5M2_X4),
                scales=g_scales[CENTRE][:, columns],
                in_=g_grouped[:, b, first:end, :, :].rearrange("p h w j -> p (h w j)"),
            )

        def quantise_half(b, half):
            if half == 0:
                quantise_grad(b, 0, ROWS_TILE)
                quantise_grad(b, ROWS_TILE, upper_rows)
            else:
                quantise_grad(b, ROWS_TILE, HEIGHT)

        def shift_grad(b, half):
            for k in TAP_ORDER[1:]:
                down, right = (k - CENTRE) * step, (k - CENTRE) * dilation
                row_lo, row_hi = inside(half * ROWS_TILE, ROWS_TILE, down, HEIGHT)
                col_lo, col_hi = inside(0, WIDTH, right, WIDTH)
                for to, source in (
                    (as_map(g_codes[k][:].bitcast(I32)), as_map(g_codes[CENTRE][:].bitcast(I32))),
                    (as_map(g_scales[k][:]), as_map(g_scales[CENTRE][:])),
                ):
                    nc.vector.tensor_copy(
                        out=to[:, b, row_lo:row_hi, col_lo:col_hi],
                        in_=source[
                            :, b, row_lo - down : row_hi - down, col_lo - right : col_hi - right
                        ],
                    )

        def regroup_weight(engine_copy, i, cols):
            engine_copy(
                out=w_grouped[i][:, :, cols, :].rearrange("p k (c e) j -> p c j e k", e=2),
                in_=w_raw[i][:].rearrange("p j (c k) -> p j c k", k=TAPS)[:, :, cols, :].rearrange(
                    "p j (c e) k -> p c j e k", e=2
                ),
            )

        def scalar_columns(i):
            return W_CHUNKS[i][1] * C_TILE * W_SCALAR_EIGHTHS[i] // 8

        def regroup_weight_scalar(i):
            regroup_weight(nc.scalar.copy, i, slice(0, scalar_columns(i)))

        def regroup_weight_vector(i):
            regroup_weight(nc.vector.tensor_copy, i, slice(scalar_columns(i), W_CHUNKS[i][1] * C_TILE))

        def quantise_weight(i):
            first, count = W_CHUNKS[i]
            columns = slice(first * C_TILE, (first + count) * C_TILE)
            for k in TAP_ORDER:
                nc.vector.quantize_mx(
                    out=w_codes[:, k, columns].bitcast(E4M3_X4),
                    scales=w_scales[:, k, columns],
                    in_=w_grouped[i][:, k, :, :].rearrange("p c j -> p (c j)"),
                )

        multiplied = []
        emptied = []
        results = {}

        def empty_oldest():
            acc, b, ct, half = multiplied[len(emptied)]
            if (b, ct) not in results:
                results[(b, ct)] = [staging.tile([C_TILE, POSITIONS], F32, name="result"), 0]
            result = results[(b, ct)][0]
            results[(b, ct)][1] += 1
            if b == BATCHES - 1 and len(emptied) % 2 == 1:
                engine_copy = nc.vector.tensor_copy
            else:
                engine_copy = nc.scalar.copy
            emptied.append(ct)
            channels = slice(ct * C_TILE, (ct + 1) * C_TILE)
            if (b, ct) != (BATCHES - 1, C_TILES - 1):
                engine_copy(out=result[:, half * N_TILE : (half + 1) * N_TILE], in_=acc[:])
                if results[(b, ct)][1] == HALVES:
                    nc.sync.dma_start(out=out_rows[b, channels, :], in_=result[:])
                return
            pieces = LAST_PIECES if len(emptied) == BATCHES * C_TILES * HALVES else 1
            width = N_TILE // pieces
            for piece in range(pieces):
                cols = slice(half * N_TILE + piece * width, half * N_TILE + (piece + 1) * width)
                engine_copy(out=result[:, cols], in_=acc[:, piece * width : (piece + 1) * width])
                nc.sync.dma_start(out=out_rows[b, channels, cols], in_=result[:, cols])

        def multiply(b, channel_tiles, half):
            columns = slice(b * POSITIONS + half * N_TILE, b * POSITIONS + (half + 1) * N_TILE)
            accs = [psum.tile([C_TILE, N_TILE], F32, name="acc") for ct in channel_tiles]
            for k in TAP_ORDER:
                for acc, ct in zip(accs, channel_tiles):
                    channels = slice(ct * C_TILE, (ct + 1) * C_TILE)
                    nc.tensor.matmul_mx(
                        out=acc[:],
                        lhsT=w_codes[:, k, channels].bitcast(E4M3_X4),
                        lhsT_scale=w_scales[:, k, channels],
                        rhs=g_codes[k][:, columns].bitcast(E5M2_X4),
                        rhs_scale=g_scales[k][:, columns],
                        start=(k == TAP_ORDER[0]),
                        stop=(k == TAP_ORDER[-1]),
                    )
            for acc, ct in zip(accs, channel_tiles):
                multiplied.append((acc, b, ct, half))
                while len(multiplied) - len(emptied) > EMPTY_LAG:
                    empty_oldest()

        load_grad(0, 0)
        load_weight(0)
        load_weight(1)
        load_grad(0, 1)
        for i in range(2, len(W_CHUNKS)):
            load_weight(i)
        for part in range(len(row_parts)):
            load_grad(1, part)
        wake_scalar()
        warm_up()
        zero_outside_the_map()

        regroup_grad_vector(0, 0)
        regroup_grad_scalar(0, 0)
        regroup_weight_scalar(0)
        regroup_weight_vector(0)
        quantise_half(0, 0)
        quantise_weight(0)
        shift_grad(0, 0)
        regroup_weight_scalar(1)
        regroup_grad_scalar(0, 1)
        regroup_weight_vector(1)
        regroup_grad_vector(0, 1)
        quantise_weight(1)
        quantise_half(0, 1)
        regroup_weight_scalar(2)
        regroup_weight_vector(2)
        shift_grad(0, 1)
        quantise_weight(2)
        def prepare_weight(i):
            regroup_weight_scalar(i)
            regroup_weight_vector(i)
            quantise_weight(i)

        for i in range(3, 2 + WEIGHTS_AHEAD):
            prepare_weight(i)
        multiply(0, (0,), 0)
        multiply(0, (1,), 0)
        multiply(0, (0, 1), 1)
        for i in range(2, len(W_CHUNKS)):
            if i + WEIGHTS_AHEAD < len(W_CHUNKS):
                prepare_weight(i + WEIGHTS_AHEAD)
            first, count = W_CHUNKS[i]
            for half in range(HALVES):
                for ct in range(first, first + count):
                    multiply(0, (ct,), half)
            if i == 3:
                for half in range(HALVES):
                    regroup_grad_scalar(1, half)
                    regroup_grad_vector(1, half)
                    quantise_half(1, half)
                    shift_grad(1, half)
        for half in range(HALVES):
            for ct in range(2):
                multiply(1, (ct,), half)
        for ct in range(2, C_TILES):
            for half in range(HALVES):
                multiply(1, (ct,), half)
        while len(emptied) < len(multiplied):
            empty_oldest()
